import numpy as np
import ml_dtypes

BF16 = ml_dtypes.bfloat16


def bf(x):
    return np.asarray(x, np.float32).astype(BF16)


def f32(x):
    return np.asarray(x, np.float32)


def f64(x):
    return np.asarray(x).astype(np.float64)


def striped(idx):
    return np.tile(idx.reshape(-1, 16).T, (8, 1))


C, S, T, L, N = 256, 256, 32, 16, 512
EPS = 1e-5


def setup_inputs():
    return {"h": f32(np.random.standard_normal((C, S))), "gain": f32(1.0 + 0.1 * np.random.standard_normal((C, 1))), "beta": f32(0.1 * np.random.standard_normal((C, 1))), "att": f32(np.random.standard_normal((1, N))), "offs": striped(np.random.permutation(np.tile(np.arange(S), 2))[:N])}


def reference(h, gain, beta, att, offs):
    idx = offs[:16].T.reshape(-1)
    r = np.maximum(f64(h), 0.0)
    mu = r.mean(axis=1, keepdims=True)
    var = np.square(r - mu).mean(axis=1, keepdims=True)
    y = (r - mu) / np.sqrt(var + EPS) * f64(gain) + f64(beta)
    e = np.exp(f64(att)).reshape(T, L)
    a = (e / e.sum(axis=1, keepdims=True)).reshape(1, N)
    return (y[:, idx] * a).reshape(C, T, L).sum(axis=2)

@@ -1,0 +1,110 @@
+import concourse.mybir as mybir
+
+F32 = mybir.dt.float32
+U16 = mybir.dt.uint16
+ALU = mybir.AluOpType
+ACT = mybir.ActivationFunctionType
+AXIS = mybir.AxisListType
+
+P = 128
+C, S, T, L, N = 256, 256, 32, 16, 512
+EPS = 1e-5
+BLOCKS = C // P
+PIECE = S
+PIECES = N // PIECE
+
+
+def tile_tag_kernel(tc, h, gain, beta, att, offs, out):
+    nc = tc.nc
+    with (
+        tc.tile_pool(name="held", bufs=1) as held,
+        tc.tile_pool(name="work", bufs=BLOCKS) as work,
+    ):
+        offsets = held.tile([P, N // 16], U16, name="offsets")
+        nc.sync.dma_start(offsets[:], offs)
+        scores = held.tile([P, N], F32, name="scores")
+        nc.scalar.dma_start(scores[:], att.broadcast_to([P, N]))
+        gains = held.tile([P, BLOCKS], F32, name="gains")
+        betas = held.tile([P, BLOCKS], F32, name="betas")
+        with nc.allow_non_contiguous_dma(reason="one float32 to a partition, 256 in all"):
+            nc.gpsimd.dma_start(gains[:], gain.rearrange("(b p) o -> p (b o)", p=P))
+            nc.gpsimd.dma_start(betas[:], beta.rearrange("(b p) o -> p (b o)", p=P))
+
+        by_team = "p (t l) -> p t l"
+        top = held.tile([P, T], F32, name="top")
+        nc.vector.tensor_reduce(
+            out=top[:], in_=scores[:].rearrange(by_team, l=L), axis=AXIS.X, op=ALU.max
+        )
+        shifted = held.tile([P, N], F32, name="shifted")
+        nc.vector.tensor_tensor(
+            out=shifted[:].rearrange(by_team, l=L),
+            in0=scores[:].rearrange(by_team, l=L),
+            in1=top[:].unsqueeze(2).to_broadcast([P, T, L]),
+            op=ALU.subtract,
+        )
+        expd = held.tile([P, N], F32, name="expd")
+        nc.scalar.activation(out=expd[:], in_=shifted[:], func=ACT.Exp)
+        den = held.tile([P, T], F32, name="den")
+        nc.vector.tensor_reduce(
+            out=den[:], in_=expd[:].rearrange(by_team, l=L), axis=AXIS.X, op=ALU.add
+        )
+        rden = held.tile([P, T], F32, name="rden")
+        nc.vector.reciprocal(out=rden[:], in_=den[:])
+        weights = held.tile([P, N], F32, name="weights")
+        nc.vector.tensor_tensor(
+            out=weights[:].rearrange(by_team, l=L),
+            in0=expd[:].rearrange(by_team, l=L),
+            in1=rden[:].unsqueeze(2).to_broadcast([P, T, L]),
+            op=ALU.mult,
+        )
+
+        for b in range(BLOCKS):
+            rows = slice(b * P, (b + 1) * P)
+            raw = work.tile([P, S], F32, name="raw")
+            nc.sync.dma_start(raw[:], h[rows, :])
+            relu = work.tile([P, S], F32, name="relu")
+            nc.vector.tensor_scalar_max(out=relu[:], in0=raw[:], scalar1=0.0)
+
+            stats = work.tile([P, 6], F32, name="stats")
+            nc.vector.bn_stats(out=stats[:], in_=relu[:])
+            mean_var = work.tile([P, 2], F32, name="mean_var")
+            nc.vector.bn_aggr(out=mean_var[:], in_=stats[:])
+            mean = mean_var[:, 0:1]
+            var = mean_var[:, 1:2]
+
+            var_eps = work.tile([P, 1], F32, name="var_eps")
+            nc.vector.tensor_scalar_add(out=var_eps[:], in0=var, scalar1=EPS)
+            std = work.tile([P, 1], F32, name="std")
+            nc.scalar.activation(out=std[:], in_=var_eps[:], func=ACT.Sqrt)
+            rstd = work.tile([P, 1], F32, name="rstd")
+            nc.vector.reciprocal(out=rstd[:], in_=std[:])
+            scale = work.tile([P, 1], F32, name="scale")
+            nc.vector.tensor_tensor(out=scale[:], in0=rstd[:], in1=gains[:, b : b + 1], op=ALU.mult)
+            mean_scaled = work.tile([P, 1], F32, name="mean_scaled")
+            nc.vector.tensor_tensor(out=mean_scaled[:], in0=mean, in1=scale[:], op=ALU.mult)
+            shift = work.tile([P, 1], F32, name="shift")
+            nc.vector.tensor_tensor(
+                out=shift[:], in0=betas[:, b : b + 1], in1=mean_scaled[:], op=ALU.subtract
+            )
+            nodes = work.tile([P, S], F32, name="nodes")
+            nc.vector.tensor_scalar(
+                out=nodes[:], in0=relu[:], scalar1=scale[:], scalar2=shift[:],
+                op0=ALU.mult, op1=ALU.add,
+            )
+
+            picked = work.tile([P, N], F32, name="picked")
+            for k in range(PIECES):
+                entries = slice(k * PIECE, (k + 1) * PIECE)
+                columns = slice(k * PIECE // 16, (k + 1) * PIECE // 16)
+                nc.vector.tensor_tensor(
+                    out=picked[:, entries],
+                    in0=nodes[:].indirect(offsets[:, columns]),
+                    in1=weights[:, entries],
+                    op=ALU.mult,
+                )
+
+            teams = work.tile([P, T], F32, name="teams")
+            nc.vector.tensor_reduce(
+                out=teams[:], in_=picked[:].rearrange(by_team, l=L), axis=AXIS.X, op=ALU.add
+            )
+            nc.sync.dma_start(out[rows, :], teams[:])

@@ -12,99 +12,104 @@ EPS = 1e-5
 BLOCKS = C // P
 PIECE = S
 PIECES = N // PIECE
+BY_TEAM = "p (t l) -> p t l"
 
 
 def tile_tag_kernel(tc, h, gain, beta, att, offs, out):
     nc = tc.nc
-    with (
-        tc.tile_pool(name="held", bufs=1) as held,
-        tc.tile_pool(name="work", bufs=BLOCKS) as work,
-    ):
+    with tc.tile_pool(name="held", bufs=1) as held:
         offsets = held.tile([P, N // 16], U16, name="offsets")
         nc.sync.dma_start(offsets[:], offs)
         scores = held.tile([P, N], F32, name="scores")
         nc.scalar.dma_start(scores[:], att.broadcast_to([P, N]))
+        raw = [held.tile([P, S], F32, name=f"raw{b}") for b in range(BLOCKS)]
+        for b in range(BLOCKS):
+            nc.sync.dma_start(raw[b][:], h[b * P : (b + 1) * P, :])
         gains = held.tile([P, BLOCKS], F32, name="gains")
         betas = held.tile([P, BLOCKS], F32, name="betas")
         with nc.allow_non_contiguous_dma(reason="one float32 to a partition, 256 in all"):
-            nc.gpsimd.dma_start(gains[:], gain.rearrange("(b p) o -> p (b o)", p=P))
-            nc.gpsimd.dma_start(betas[:], beta.rearrange("(b p) o -> p (b o)", p=P))
+            nc.scalar.dma_start(gains[:], gain.rearrange("(b p) o -> p (b o)", p=P))
+            nc.scalar.dma_start(betas[:], beta.rearrange("(b p) o -> p (b o)", p=P))
+        minus_half = held.tile([P, BLOCKS], F32, name="minus_half")
+        nc.gpsimd.memset(minus_half[:], -0.5)
 
-        by_team = "p (t l) -> p t l"
         top = held.tile([P, T], F32, name="top")
-        nc.vector.tensor_reduce(
-            out=top[:], in_=scores[:].rearrange(by_team, l=L), axis=AXIS.X, op=ALU.max
-        )
         shifted = held.tile([P, N], F32, name="shifted")
-        nc.vector.tensor_tensor(
-            out=shifted[:].rearrange(by_team, l=L),
-            in0=scores[:].rearrange(by_team, l=L),
-            in1=top[:].unsqueeze(2).to_broadcast([P, T, L]),
-            op=ALU.subtract,
-        )
         expd = held.tile([P, N], F32, name="expd")
-        nc.scalar.activation(out=expd[:], in_=shifted[:], func=ACT.Exp)
-        den = held.tile([P, T], F32, name="den")
-        nc.vector.tensor_reduce(
-            out=den[:], in_=expd[:].rearrange(by_team, l=L), axis=AXIS.X, op=ALU.add
-        )
-        rden = held.tile([P, T], F32, name="rden")
-        nc.vector.reciprocal(out=rden[:], in_=den[:])
-        weights = held.tile([P, N], F32, name="weights")
-        nc.vector.tensor_tensor(
-            out=weights[:].rearrange(by_team, l=L),
-            in0=expd[:].rearrange(by_team, l=L),
-            in1=rden[:].unsqueeze(2).to_broadcast([P, T, L]),
-            op=ALU.mult,
-        )
-
-        for b in range(BLOCKS):
-            rows = slice(b * P, (b + 1) * P)
-            raw = work.tile([P, S], F32, name="raw")
-            nc.sync.dma_start(raw[:], h[rows, :])
-            relu = work.tile([P, S], F32, name="relu")
-            nc.vector.tensor_scalar_max(out=relu[:], in0=raw[:], scalar1=0.0)
-
-            stats = work.tile([P, 6], F32, name="stats")
-            nc.vector.bn_stats(out=stats[:], in_=relu[:])
-            mean_var = work.tile([P, 2], F32, name="mean_var")
-            nc.vector.bn_aggr(out=mean_var[:], in_=stats[:])
-            mean = mean_var[:, 0:1]
-            var = mean_var[:, 1:2]
-
-            var_eps = work.tile([P, 1], F32, name="var_eps")
-            nc.vector.tensor_scalar_add(out=var_eps[:], in0=var, scalar1=EPS)
-            std = work.tile([P, 1], F32, name="std")
-            nc.scalar.activation(out=std[:], in_=var_eps[:], func=ACT.Sqrt)
-            rstd = work.tile([P, 1], F32, name="rstd")
-            nc.vector.reciprocal(out=rstd[:], in_=std[:])
-            scale = work.tile([P, 1], F32, name="scale")
-            nc.vector.tensor_tensor(out=scale[:], in0=rstd[:], in1=gains[:, b : b + 1], op=ALU.mult)
-            mean_scaled = work.tile([P, 1], F32, name="mean_scaled")
-            nc.vector.tensor_tensor(out=mean_scaled[:], in0=mean, in1=scale[:], op=ALU.mult)
-            shift = work.tile([P, 1], F32, name="shift")
+        relu = [held.tile([P, S], F32, name=f"relu{b}") for b in range(BLOCKS)]
+        sums = held.tile([P, BLOCKS], F32, name="sums")
+        for k in range(PIECES):
+            entries = slice(k * PIECE, (k + 1) * PIECE)
+            teams = slice(k * PIECE // L, (k + 1) * PIECE // L)
+            nc.vector.tensor_reduce(
+                out=top[:, teams], in_=scores[:, entries].rearrange(BY_TEAM, l=L),
+                axis=AXIS.X, op=ALU.max,
+            )
             nc.vector.tensor_tensor(
-                out=shift[:], in0=betas[:, b : b + 1], in1=mean_scaled[:], op=ALU.subtract
+                out=shifted[:, entries].rearrange(BY_TEAM, l=L),
+                in0=scores[:, entries].rearrange(BY_TEAM, l=L),
+                in1=top[:, teams].unsqueeze(2).to_broadcast([P, PIECE // L, L]),
+                op=ALU.subtract,
             )
-            nodes = work.tile([P, S], F32, name="nodes")
-            nc.vector.tensor_scalar(
-                out=nodes[:], in0=relu[:], scalar1=scale[:], scalar2=shift[:],
-                op0=ALU.mult, op1=ALU.add,
+        for b in range(BLOCKS):
+            nc.scalar.activation(
+                out=relu[b][:], in_=raw[b][:], func=ACT.Relu, accum_out=sums[:, b : b + 1]
             )
+            entries = slice(b * PIECE, (b + 1) * PIECE)
+            nc.scalar.activation(out=expd[:, entries], in_=shifted[:, entries], func=ACT.Exp)
 
-            picked = work.tile([P, N], F32, name="picked")
+        minus_mean = held.tile([P, BLOCKS], F32, name="minus_mean")
+        nc.gpsimd.tensor_scalar_mul(out=minus_mean[:], in0=sums[:], scalar1=-1.0 / S)
+        squares = held.tile([P, BLOCKS], F32, name="squares")
+        for b in range(BLOCKS):
+            centred_sq = held.tile([P, S], F32, name=f"centred_sq{b}")
+            nc.scalar.activation(
+                out=centred_sq[:], in_=relu[b][:], func=ACT.Square,
+                bias=minus_mean[:, b : b + 1], accum_out=squares[:, b : b + 1],
+            )
+        var_eps = held.tile([P, BLOCKS], F32, name="var_eps")
+        nc.gpsimd.tensor_scalar(
+            out=var_eps[:], in0=squares[:], scalar1=1.0 / S, scalar2=EPS,
+            op0=ALU.mult, op1=ALU.add,
+        )
+        rstd = held.tile([P, BLOCKS], F32, name="rstd")
+        nc.gpsimd.tensor_tensor(out=rstd[:], in0=var_eps[:], in1=minus_half[:], op=ALU.pow)
+        scale = held.tile([P, BLOCKS], F32, name="scale")
+        nc.gpsimd.tensor_tensor(out=scale[:], in0=rstd[:], in1=gains[:], op=ALU.mult)
+        shift = held.tile([P, BLOCKS], F32, name="shift")
+        nc.gpsimd.tensor_tensor(out=shift[:], in0=minus_mean[:], in1=scale[:], op=ALU.mult)
+        nc.gpsimd.tensor_tensor(out=shift[:], in0=shift[:], in1=betas[:], op=ALU.add)
+
+        summed = []
+        for b in range(BLOCKS):
+            picked = held.tile([P, N], F32, name=f"picked{b}")
             for k in range(PIECES):
                 entries = slice(k * PIECE, (k + 1) * PIECE)
                 columns = slice(k * PIECE // 16, (k + 1) * PIECE // 16)
                 nc.vector.tensor_tensor(
                     out=picked[:, entries],
-                    in0=nodes[:].indirect(offsets[:, columns]),
-                    in1=weights[:, entries],
+                    in0=relu[b][:].indirect(offsets[:, columns]),
+                    in1=expd[:, entries],
                     op=ALU.mult,
                 )
-
-            teams = work.tile([P, T], F32, name="teams")
+            summed.append(held.tile([P, T], F32, name=f"summed{b}"))
             nc.vector.tensor_reduce(
-                out=teams[:], in_=picked[:].rearrange(by_team, l=L), axis=AXIS.X, op=ALU.add
+                out=summed[b][:], in_=picked[:].rearrange(BY_TEAM, l=L), axis=AXIS.X, op=ALU.add
             )
-            nc.sync.dma_start(out[rows, :], teams[:])
+
+        den = held.tile([P, T], F32, name="den")
+        nc.vector.tensor_reduce(
+            out=den[:], in_=expd[:].rearrange(BY_TEAM, l=L), axis=AXIS.X, op=ALU.add
+        )
+        rden = held.tile([P, T], F32, name="rden")
+        nc.vector.reciprocal(out=rden[:], in_=den[:])
+
+        for b in range(BLOCKS):
+            result = held.tile([P, T], F32, name=f"result{b}")
+            nc.vector.scalar_tensor_tensor(
+                out=result[:], in0=summed[b][:], scalar=scale[:, b : b + 1], in1=rden[:],
+                op0=ALU.mult, op1=ALU.mult,
+            )
+            nc.vector.tensor_scalar_add(out=result[:], in0=result[:], scalar1=shift[:, b : b + 1])
+            queue = nc.sync if b == 0 else nc.scalar
+            queue.dma_start(out[b * P : (b + 1) * P, :], result[:])

@@ -1,4 +1,5 @@
 import concourse.mybir as mybir
+from concourse.masks import make_identity
 
 F32 = mybir.dt.float32
 U16 = mybir.dt.uint16
@@ -12,16 +13,22 @@ EPS = 1e-5
 BLOCKS = C // P
 PIECE = S
 PIECES = N // PIECE
+PIECE_TEAMS = PIECE // L
 BY_TEAM = "p (t l) -> p t l"
 
 
 def tile_tag_kernel(tc, h, gain, beta, att, offs, out):
     nc = tc.nc
-    with tc.tile_pool(name="held", bufs=1) as held:
+    with (
+        tc.tile_pool(name="held", bufs=1) as held,
+        tc.psum_pool(name="psum", bufs=1) as psum,
+    ):
         offsets = held.tile([P, N // 16], U16, name="offsets")
         nc.sync.dma_start(offsets[:], offs)
         scores = held.tile([P, N], F32, name="scores")
         nc.scalar.dma_start(scores[:], att.broadcast_to([P, N]))
+        team_scores = held.tile([T, L], F32, name="team_scores")
+        nc.sync.dma_start(team_scores[:], att.rearrange("o (t l) -> (o t) l", l=L))
         raw = [held.tile([P, S], F32, name=f"raw{b}") for b in range(BLOCKS)]
         for b in range(BLOCKS):
             nc.sync.dma_start(raw[b][:], h[b * P : (b + 1) * P, :])
@@ -30,36 +37,66 @@ def tile_tag_kernel(tc, h, gain, beta, att, offs, out):
         with nc.allow_non_contiguous_dma(reason="one float32 to a partition, 256 in all"):
             nc.scalar.dma_start(gains[:], gain.rearrange("(b p) o -> p (b o)", p=P))
             nc.scalar.dma_start(betas[:], beta.rearrange("(b p) o -> p (b o)", p=P))
+
         minus_half = held.tile([P, BLOCKS], F32, name="minus_half")
         nc.gpsimd.memset(minus_half[:], -0.5)
+        eps = held.tile([P, 1], F32, name="eps")
+        nc.gpsimd.memset(eps[:], EPS)
+        ones = held.tile([T, P], F32, name="ones")
+        nc.gpsimd.memset(ones[:], 1.0)
+        identity = held.tile([T, T], F32, name="identity")
+        make_identity(nc, identity[:])
+
+        team_minus_top = held.tile([T, 1], F32, name="team_minus_top")
+        nc.vector.tensor_reduce(
+            out=team_minus_top[:], in_=team_scores[:], axis=AXIS.X, op=ALU.max, negate=True
+        )
+        team_expd = held.tile([T, L], F32, name="team_expd")
+        team_den = held.tile([T, 1], F32, name="team_den")
+        nc.scalar.activation(
+            out=team_expd[:], in_=team_scores[:], func=ACT.Exp,
+            bias=team_minus_top[:], accum_out=team_den[:],
+        )
 
         top = held.tile([P, T], F32, name="top")
         shifted = held.tile([P, N], F32, name="shifted")
         expd = held.tile([P, N], F32, name="expd")
-        relu = [held.tile([P, S], F32, name=f"relu{b}") for b in range(BLOCKS)]
-        sums = held.tile([P, BLOCKS], F32, name="sums")
         for k in range(PIECES):
             entries = slice(k * PIECE, (k + 1) * PIECE)
-            teams = slice(k * PIECE // L, (k + 1) * PIECE // L)
+            teams = slice(k * PIECE_TEAMS, (k + 1) * PIECE_TEAMS)
             nc.vector.tensor_reduce(
                 out=top[:, teams], in_=scores[:, entries].rearrange(BY_TEAM, l=L),
                 axis=AXIS.X, op=ALU.max,
             )
+        for k in range(PIECES):
+            entries = slice(k * PIECE, (k + 1) * PIECE)
+            teams = slice(k * PIECE_TEAMS, (k + 1) * PIECE_TEAMS)
             nc.vector.tensor_tensor(
                 out=shifted[:, entries].rearrange(BY_TEAM, l=L),
                 in0=scores[:, entries].rearrange(BY_TEAM, l=L),
-                in1=top[:, teams].unsqueeze(2).to_broadcast([P, PIECE // L, L]),
+                in1=top[:, teams].unsqueeze(2).to_broadcast([P, PIECE_TEAMS, L]),
                 op=ALU.subtract,
             )
+
+        relu = [held.tile([P, S], F32, name=f"relu{b}") for b in range(BLOCKS)]
+        sums = held.tile([P, BLOCKS], F32, name="sums")
         for b in range(BLOCKS):
             nc.scalar.activation(
                 out=relu[b][:], in_=raw[b][:], func=ACT.Relu, accum_out=sums[:, b : b + 1]
             )
-            entries = slice(b * PIECE, (b + 1) * PIECE)
+        for k in range(PIECES):
+            entries = slice(k * PIECE, (k + 1) * PIECE)
             nc.scalar.activation(out=expd[:, entries], in_=shifted[:, entries], func=ACT.Exp)
 
+        team_rden = held.tile([T, 1], F32, name="team_rden")
+        nc.vector.reciprocal(out=team_rden[:], in_=team_den[:])
+        diagonal = held.tile([T, T], F32, name="diagonal")
+        nc.scalar.activation(out=diagonal[:], in_=identity[:], func=ACT.Copy, scale=team_rden[:])
+        rden = psum.tile([P, T], F32, name="rden")
+        nc.tensor.matmul(rden[:], ones[:], diagonal[:], start=True, stop=True)
+
         minus_mean = held.tile([P, BLOCKS], F32, name="minus_mean")
-        nc.gpsimd.tensor_scalar_mul(out=minus_mean[:], in0=sums[:], scalar1=-1.0 / S)
+        nc.scalar.mul(out=minus_mean[:], in_=sums[:], mul=-1.0 / S)
         squares = held.tile([P, BLOCKS], F32, name="squares")
         for b in range(BLOCKS):
             centred_sq = held.tile([P, S], F32, name=f"centred_sq{b}")
@@ -68,48 +105,53 @@ def tile_tag_kernel(tc, h, gain, beta, att, offs, out):
                 bias=minus_mean[:, b : b + 1], accum_out=squares[:, b : b + 1],
             )
         var_eps = held.tile([P, BLOCKS], F32, name="var_eps")
-        nc.gpsimd.tensor_scalar(
-            out=var_eps[:], in0=squares[:], scalar1=1.0 / S, scalar2=EPS,
-            op0=ALU.mult, op1=ALU.add,
+        nc.scalar.activation(
+            out=var_eps[:], in_=squares[:], func=ACT.Identity, scale=1.0 / S, bias=eps[:]
         )
         rstd = held.tile([P, BLOCKS], F32, name="rstd")
         nc.gpsimd.tensor_tensor(out=rstd[:], in0=var_eps[:], in1=minus_half[:], op=ALU.pow)
         scale = held.tile([P, BLOCKS], F32, name="scale")
-        nc.gpsimd.tensor_tensor(out=scale[:], in0=rstd[:], in1=gains[:], op=ALU.mult)
         shift = held.tile([P, BLOCKS], F32, name="shift")
-        nc.gpsimd.tensor_tensor(out=shift[:], in0=minus_mean[:], in1=scale[:], op=ALU.mult)
-        nc.gpsimd.tensor_tensor(out=shift[:], in0=shift[:], in1=betas[:], op=ALU.add)
-
-        summed = []
+        factor = held.tile([P, BLOCKS, T], F32, name="factor")
         for b in range(BLOCKS):
-            picked = held.tile([P, N], F32, name=f"picked{b}")
-            for k in range(PIECES):
-                entries = slice(k * PIECE, (k + 1) * PIECE)
-                columns = slice(k * PIECE // 16, (k + 1) * PIECE // 16)
-                nc.vector.tensor_tensor(
-                    out=picked[:, entries],
-                    in0=relu[b][:].indirect(offsets[:, columns]),
-                    in1=expd[:, entries],
-                    op=ALU.mult,
-                )
-            summed.append(held.tile([P, T], F32, name=f"summed{b}"))
+            block = slice(b, b + 1)
+            nc.scalar.activation(
+                out=scale[:, block], in_=rstd[:, block], func=ACT.Copy, scale=gains[:, block]
+            )
+            nc.scalar.activation(
+                out=factor[:, b, :], in_=rden[:], func=ACT.Copy, scale=scale[:, block]
+            )
+            nc.scalar.activation(
+                out=shift[:, block], in_=minus_mean[:, block], func=ACT.Identity,
+                scale=scale[:, block], bias=betas[:, block],
+            )
+
+        picked = held.tile([P, BLOCKS, N], F32, name="picked")
+        summed = held.tile([P, BLOCKS, T], F32, name="summed")
+
+        def sum_teams(b, k):
             nc.vector.tensor_reduce(
-                out=summed[b][:], in_=picked[:].rearrange(BY_TEAM, l=L), axis=AXIS.X, op=ALU.add
+                out=summed[:, b, k * PIECE_TEAMS : (k + 1) * PIECE_TEAMS],
+                in_=picked[:, b, k * PIECE : (k + 1) * PIECE].rearrange(BY_TEAM, l=L),
+                axis=AXIS.X, op=ALU.add,
             )
 
-        den = held.tile([P, T], F32, name="den")
-        nc.vector.tensor_reduce(
-            out=den[:], in_=expd[:].rearrange(BY_TEAM, l=L), axis=AXIS.X, op=ALU.add
+        steps = [(b, k) for b in range(BLOCKS) for k in range(PIECES)]
+        for i, (b, k) in enumerate(steps):
+            nc.vector.tensor_tensor(
+                out=picked[:, b, k * PIECE : (k + 1) * PIECE],
+                in0=relu[b][:].indirect(offsets[:, k * PIECE // 16 : (k + 1) * PIECE // 16]),
+                in1=expd[:, k * PIECE : (k + 1) * PIECE],
+                op=ALU.mult,
+            )
+            if i > 0:
+                sum_teams(*steps[i - 1])
+        sum_teams(*steps[-1])
+
+        result = held.tile([P, BLOCKS, T], F32, name="result")
+        nc.vector.tensor_tensor(out=result[:], in0=summed[:], in1=factor[:], op=ALU.mult)
+        nc.vector.tensor_tensor(
+            out=result[:], in0=result[:],
+            in1=shift[:].unsqueeze(2).to_broadcast([P, BLOCKS, T]), op=ALU.add,
         )
-        rden = held.tile([P, T], F32, name="rden")
-        nc.vector.reciprocal(out=rden[:], in_=den[:])
-
-        for b in range(BLOCKS):
-            result = held.tile([P, T], F32, name=f"result{b}")
-            nc.vector.scalar_tensor_tensor(
-                out=result[:], in0=summed[b][:], scalar=scale[:, b : b + 1], in1=rden[:],
-                op0=ALU.mult, op1=ALU.mult,
-            )
-            nc.vector.tensor_scalar_add(out=result[:], in0=result[:], scalar1=shift[:, b : b + 1])
-            queue = nc.sync if b == 0 else nc.scalar
-            queue.dma_start(out[b * P : (b + 1) * P, :], result[:])
+        nc.sync.dma_start(out.rearrange("(b p) t -> p b t", p=P), result[:])

@@ -60,7 +60,6 @@ def tile_tag_kernel(tc, h, gain, beta, att, offs, out):
 
         top = held.tile([P, T], F32, name="top")
         shifted = held.tile([P, N], F32, name="shifted")
-        expd = held.tile([P, N], F32, name="expd")
         for k in range(PIECES):
             entries = slice(k * PIECE, (k + 1) * PIECE)
             teams = slice(k * PIECE_TEAMS, (k + 1) * PIECE_TEAMS)
@@ -84,9 +83,13 @@ def tile_tag_kernel(tc, h, gain, beta, att, offs, out):
             nc.scalar.activation(
                 out=relu[b][:], in_=raw[b][:], func=ACT.Relu, accum_out=sums[:, b : b + 1]
             )
+        expd = held.tile([P, N], F32, name="expd")
         for k in range(PIECES):
             entries = slice(k * PIECE, (k + 1) * PIECE)
             nc.scalar.activation(out=expd[:, entries], in_=shifted[:, entries], func=ACT.Exp)
+
+        minus_mean = held.tile([P, BLOCKS], F32, name="minus_mean")
+        nc.scalar.mul(out=minus_mean[:], in_=sums[:], mul=-1.0 / S)
 
         team_rden = held.tile([T, 1], F32, name="team_rden")
         nc.vector.reciprocal(out=team_rden[:], in_=team_den[:])
@@ -95,8 +98,6 @@ def tile_tag_kernel(tc, h, gain, beta, att, offs, out):
         rden = psum.tile([P, T], F32, name="rden")
         nc.tensor.matmul(rden[:], ones[:], diagonal[:], start=True, stop=True)
 
-        minus_mean = held.tile([P, BLOCKS], F32, name="minus_mean")
-        nc.scalar.mul(out=minus_mean[:], in_=sums[:], mul=-1.0 / S)
         squares = held.tile([P, BLOCKS], F32, name="squares")
         for b in range(BLOCKS):
             centred_sq = held.tile([P, S], F32, name=f"centred_sq{b}")
@@ -104,26 +105,20 @@ def tile_tag_kernel(tc, h, gain, beta, att, offs, out):
                 out=centred_sq[:], in_=relu[b][:], func=ACT.Square,
                 bias=minus_mean[:, b : b + 1], accum_out=squares[:, b : b + 1],
             )
+        rstd = held.tile([P, BLOCKS], F32, name="rstd")
+        minus_mean_gain = held.tile([P, BLOCKS], F32, name="minus_mean_gain")
         var_eps = held.tile([P, BLOCKS], F32, name="var_eps")
         nc.scalar.activation(
             out=var_eps[:], in_=squares[:], func=ACT.Identity, scale=1.0 / S, bias=eps[:]
         )
-        rstd = held.tile([P, BLOCKS], F32, name="rstd")
+        nc.gpsimd.tensor_tensor(out=minus_mean_gain[:], in0=minus_mean[:], in1=gains[:], op=ALU.mult)
         nc.gpsimd.tensor_tensor(out=rstd[:], in0=var_eps[:], in1=minus_half[:], op=ALU.pow)
-        scale = held.tile([P, BLOCKS], F32, name="scale")
         shift = held.tile([P, BLOCKS], F32, name="shift")
-        factor = held.tile([P, BLOCKS, T], F32, name="factor")
         for b in range(BLOCKS):
             block = slice(b, b + 1)
             nc.scalar.activation(
-                out=scale[:, block], in_=rstd[:, block], func=ACT.Copy, scale=gains[:, block]
-            )
-            nc.scalar.activation(
-                out=factor[:, b, :], in_=rden[:], func=ACT.Copy, scale=scale[:, block]
-            )
-            nc.scalar.activation(
-                out=shift[:, block], in_=minus_mean[:, block], func=ACT.Identity,
-                scale=scale[:, block], bias=betas[:, block],
+                out=shift[:, block], in_=rstd[:, block], func=ACT.Identity,
+                scale=minus_mean_gain[:, block], bias=betas[:, block],
             )
 
         picked = held.tile([P, BLOCKS, N], F32, name="picked")
@@ -148,10 +143,17 @@ def tile_tag_kernel(tc, h, gain, beta, att, offs, out):
                 sum_teams(*steps[i - 1])
         sum_teams(*steps[-1])
 
+        normed = held.tile([P, BLOCKS, T], F32, name="normed")
         result = held.tile([P, BLOCKS, T], F32, name="result")
-        nc.vector.tensor_tensor(out=result[:], in0=summed[:], in1=factor[:], op=ALU.mult)
-        nc.vector.tensor_tensor(
-            out=result[:], in0=result[:],
-            in1=shift[:].unsqueeze(2).to_broadcast([P, BLOCKS, T]), op=ALU.add,
-        )
+        for b in range(BLOCKS):
+            nc.vector.scalar_tensor_tensor(
+                out=normed[:, b, :], in0=summed[:, b, :], scalar=rstd[:, b : b + 1], in1=rden[:],
+                op0=ALU.mult, op1=ALU.mult,
+            )
+        for b in range(BLOCKS):
+            nc.vector.tensor_scalar(
+                out=result[:, b, :], in0=normed[:, b, :],
+                scalar1=gains[:, b : b + 1], scalar2=shift[:, b : b + 1],
+                op0=ALU.mult, op1=ALU.add,
+            )
         nc.sync.dma_start(out.rearrange("(b p) t -> p b t", p=P), result[:])

@@ -38,8 +38,6 @@ def tile_tag_kernel(tc, h, gain, beta, att, offs, out):
             nc.scalar.dma_start(gains[:], gain.rearrange("(b p) o -> p (b o)", p=P))
             nc.scalar.dma_start(betas[:], beta.rearrange("(b p) o -> p (b o)", p=P))
 
-        minus_half = held.tile([P, BLOCKS], F32, name="minus_half")
-        nc.gpsimd.memset(minus_half[:], -0.5)
         eps = held.tile([P, 1], F32, name="eps")
         nc.gpsimd.memset(eps[:], EPS)
         ones = held.tile([T, P], F32, name="ones")
@@ -107,12 +105,15 @@ def tile_tag_kernel(tc, h, gain, beta, att, offs, out):
             )
         rstd = held.tile([P, BLOCKS], F32, name="rstd")
         minus_mean_gain = held.tile([P, BLOCKS], F32, name="minus_mean_gain")
-        var_eps = held.tile([P, BLOCKS], F32, name="var_eps")
         nc.scalar.activation(
-            out=var_eps[:], in_=squares[:], func=ACT.Identity, scale=1.0 / S, bias=eps[:]
+            out=rstd[:], in_=squares[:], func=ACT.Abs_reciprocal_sqrt, scale=1.0 / S, bias=eps[:]
         )
-        nc.gpsimd.tensor_tensor(out=minus_mean_gain[:], in0=minus_mean[:], in1=gains[:], op=ALU.mult)
-        nc.gpsimd.tensor_tensor(out=rstd[:], in0=var_eps[:], in1=minus_half[:], op=ALU.pow)
+        for b in range(BLOCKS):
+            block = slice(b, b + 1)
+            nc.scalar.activation(
+                out=minus_mean_gain[:, block], in_=minus_mean[:, block], func=ACT.Copy,
+                scale=gains[:, block],
+            )
         shift = held.tile([P, BLOCKS], F32, name="shift")
         for b in range(BLOCKS):
             block = slice(b, b + 1)

@@ -26,7 +26,9 @@ def tile_tag_kernel(tc, h, gain, beta, att, offs, out):
         offsets = held.tile([P, N // 16], U16, name="offsets")
         nc.sync.dma_start(offsets[:], offs)
         scores = held.tile([P, N], F32, name="scores")
-        nc.scalar.dma_start(scores[:], att.broadcast_to([P, N]))
+        for k in range(PIECES):
+            entries = slice(k * PIECE, (k + 1) * PIECE)
+            nc.scalar.dma_start(scores[:, entries], att[:, entries].broadcast_to([P, PIECE]))
         team_scores = held.tile([T, L], F32, name="team_scores")
         nc.sync.dma_start(team_scores[:], att.rearrange("o (t l) -> (o t) l", l=L))
         raw = [held.tile([P, S], F32, name=f"raw{b}") for b in range(BLOCKS)]
@@ -38,6 +40,8 @@ def tile_tag_kernel(tc, h, gain, beta, att, offs, out):
             nc.scalar.dma_start(gains[:], gain.rearrange("(b p) o -> p (b o)", p=P))
             nc.scalar.dma_start(betas[:], beta.rearrange("(b p) o -> p (b o)", p=P))
 
+        minus_half = held.tile([P, BLOCKS], F32, name="minus_half")
+        nc.gpsimd.memset(minus_half[:], -0.5)
         eps = held.tile([P, 1], F32, name="eps")
         nc.gpsimd.memset(eps[:], EPS)
         ones = held.tile([T, P], F32, name="ones")
@@ -105,15 +109,12 @@ def tile_tag_kernel(tc, h, gain, beta, att, offs, out):
             )
         rstd = held.tile([P, BLOCKS], F32, name="rstd")
         minus_mean_gain = held.tile([P, BLOCKS], F32, name="minus_mean_gain")
+        var_eps = held.tile([P, BLOCKS], F32, name="var_eps")
         nc.scalar.activation(
-            out=rstd[:], in_=squares[:], func=ACT.Abs_reciprocal_sqrt, scale=1.0 / S, bias=eps[:]
+            out=var_eps[:], in_=squares[:], func=ACT.Identity, scale=1.0 / S, bias=eps[:]
         )
-        for b in range(BLOCKS):
-            block = slice(b, b + 1)
-            nc.scalar.activation(
-                out=minus_mean_gain[:, block], in_=minus_mean[:, block], func=ACT.Copy,
-                scale=gains[:, block],
-            )
+        nc.gpsimd.tensor_tensor(out=minus_mean_gain[:], in0=minus_mean[:], in1=gains[:], op=ALU.mult)
+        nc.gpsimd.tensor_tensor(out=rstd[:], in0=var_eps[:], in1=minus_half[:], op=ALU.pow)
         shift = held.tile([P, BLOCKS], F32, name="shift")
         for b in range(BLOCKS):
             block = slice(b, b + 1)

@@ -26,14 +26,12 @@ def tile_tag_kernel(tc, h, gain, beta, att, offs, out):
         offsets = held.tile([P, N // 16], U16, name="offsets")
         nc.sync.dma_start(offsets[:], offs)
         scores = held.tile([P, N], F32, name="scores")
-        for k in range(PIECES):
-            entries = slice(k * PIECE, (k + 1) * PIECE)
-            nc.scalar.dma_start(scores[:, entries], att[:, entries].broadcast_to([P, PIECE]))
-        team_scores = held.tile([T, L], F32, name="team_scores")
-        nc.sync.dma_start(team_scores[:], att.rearrange("o (t l) -> (o t) l", l=L))
+        nc.scalar.dma_start(scores[:], att.broadcast_to([P, N]))
         raw = [held.tile([P, S], F32, name=f"raw{b}") for b in range(BLOCKS)]
         for b in range(BLOCKS):
             nc.sync.dma_start(raw[b][:], h[b * P : (b + 1) * P, :])
+        team_scores = held.tile([T, L], F32, name="team_scores")
+        nc.sync.dma_start(team_scores[:], att.rearrange("o (t l) -> (o t) l", l=L))
         gains = held.tile([P, BLOCKS], F32, name="gains")
         betas = held.tile([P, BLOCKS], F32, name="betas")
         with nc.allow_non_contiguous_dma(reason="one float32 to a partition, 256 in all"):
@@ -48,17 +46,6 @@ def tile_tag_kernel(tc, h, gain, beta, att, offs, out):
         nc.gpsimd.memset(ones[:], 1.0)
         identity = held.tile([T, T], F32, name="identity")
         make_identity(nc, identity[:])
-
-        team_minus_top = held.tile([T, 1], F32, name="team_minus_top")
-        nc.vector.tensor_reduce(
-            out=team_minus_top[:], in_=team_scores[:], axis=AXIS.X, op=ALU.max, negate=True
-        )
-        team_expd = held.tile([T, L], F32, name="team_expd")
-        team_den = held.tile([T, 1], F32, name="team_den")
-        nc.scalar.activation(
-            out=team_expd[:], in_=team_scores[:], func=ACT.Exp,
-            bias=team_minus_top[:], accum_out=team_den[:],
-        )
 
         top = held.tile([P, T], F32, name="top")
         shifted = held.tile([P, N], F32, name="shifted")
@@ -89,6 +76,17 @@ def tile_tag_kernel(tc, h, gain, beta, att, offs, out):
         for k in range(PIECES):
             entries = slice(k * PIECE, (k + 1) * PIECE)
             nc.scalar.activation(out=expd[:, entries], in_=shifted[:, entries], func=ACT.Exp)
+
+        team_minus_top = held.tile([T, 1], F32, name="team_minus_top")
+        nc.vector.tensor_reduce(
+            out=team_minus_top[:], in_=team_scores[:], axis=AXIS.X, op=ALU.max, negate=True
+        )
+        team_expd = held.tile([T, L], F32, name="team_expd")
+        team_den = held.tile([T, 1], F32, name="team_den")
+        nc.scalar.activation(
+            out=team_expd[:], in_=team_scores[:], func=ACT.Exp,
+            bias=team_minus_top[:], accum_out=team_den[:],
+        )
 
         minus_mean = held.tile([P, BLOCKS], F32, name="minus_mean")
         nc.scalar.mul(out=minus_mean[:], in_=sums[:], mul=-1.0 / S)

@@ -29,14 +29,13 @@ def tile_tag_kernel(tc, h, gain, beta, att, offs, out):
         nc.scalar.dma_start(scores[:], att.broadcast_to([P, N]))
         raw = [held.tile([P, S], F32, name=f"raw{b}") for b in range(BLOCKS)]
         for b in range(BLOCKS):
-            nc.sync.dma_start(raw[b][:], h[b * P : (b + 1) * P, :])
+            nc.sync.dma_start(raw[b][:], h.rearrange("(p b) s -> b p s", b=BLOCKS)[b])
         team_scores = held.tile([T, L], F32, name="team_scores")
         nc.sync.dma_start(team_scores[:], att.rearrange("o (t l) -> (o t) l", l=L))
         gains = held.tile([P, BLOCKS], F32, name="gains")
         betas = held.tile([P, BLOCKS], F32, name="betas")
-        with nc.allow_non_contiguous_dma(reason="one float32 to a partition, 256 in all"):
-            nc.scalar.dma_start(gains[:], gain.rearrange("(b p) o -> p (b o)", p=P))
-            nc.scalar.dma_start(betas[:], beta.rearrange("(b p) o -> p (b o)", p=P))
+        nc.scalar.dma_start(gains[:], gain.rearrange("(p b) o -> p (b o)", b=BLOCKS))
+        nc.scalar.dma_start(betas[:], beta.rearrange("(p b) o -> p (b o)", b=BLOCKS))
 
         minus_half = held.tile([P, BLOCKS], F32, name="minus_half")
         nc.gpsimd.memset(minus_half[:], -0.5)
@@ -156,4 +155,4 @@ def tile_tag_kernel(tc, h, gain, beta, att, offs, out):
                 scalar1=gains[:, b : b + 1], scalar2=shift[:, b : b + 1],
                 op0=ALU.mult, op1=ALU.add,
             )
-        nc.sync.dma_start(out.rearrange("(b p) t -> p b t", p=P), result[:])
+        nc.sync.dma_start(out.rearrange("(p b) t -> p b t", b=BLOCKS), result[:])

@@ -26,7 +26,7 @@ def tile_tag_kernel(tc, h, gain, beta, att, offs, out):
         offsets = held.tile([P, N // 16], U16, name="offsets")
         nc.sync.dma_start(offsets[:], offs)
         scores = held.tile([P, N], F32, name="scores")
-        nc.scalar.dma_start(scores[:], att.broadcast_to([P, N]))
+        nc.sync.dma_start(scores[:], att.broadcast_to([P, N]))
         raw = [held.tile([P, S], F32, name=f"raw{b}") for b in range(BLOCKS)]
         for b in range(BLOCKS):
             nc.sync.dma_start(raw[b][:], h.rearrange("(p b) s -> b p s", b=BLOCKS)[b])
@@ -34,8 +34,8 @@ def tile_tag_kernel(tc, h, gain, beta, att, offs, out):
         nc.sync.dma_start(team_scores[:], att.rearrange("o (t l) -> (o t) l", l=L))
         gains = held.tile([P, BLOCKS], F32, name="gains")
         betas = held.tile([P, BLOCKS], F32, name="betas")
-        nc.scalar.dma_start(gains[:], gain.rearrange("(p b) o -> p (b o)", b=BLOCKS))
-        nc.scalar.dma_start(betas[:], beta.rearrange("(p b) o -> p (b o)", b=BLOCKS))
+        nc.sync.dma_start(gains[:], gain.rearrange("(p b) o -> p (b o)", b=BLOCKS))
+        nc.sync.dma_start(betas[:], beta.rearrange("(p b) o -> p (b o)", b=BLOCKS))
 
         minus_half = held.tile([P, BLOCKS], F32, name="minus_half")
         nc.gpsimd.memset(minus_half[:], -0.5)

@@ -14,6 +14,8 @@ BLOCKS = C // P
 PIECE = S
 PIECES = N // PIECE
 PIECE_TEAMS = PIECE // L
+W_PIECE = 128
+W_TEAMS = W_PIECE // L
 BY_TEAM = "p (t l) -> p t l"
 
 
@@ -24,12 +26,12 @@ def tile_tag_kernel(tc, h, gain, beta, att, offs, out):
         tc.psum_pool(name="psum", bufs=1) as psum,
     ):
         offsets = held.tile([P, N // 16], U16, name="offsets")
-        nc.sync.dma_start(offsets[:], offs)
         scores = held.tile([P, N], F32, name="scores")
         nc.sync.dma_start(scores[:], att.broadcast_to([P, N]))
         raw = [held.tile([P, S], F32, name=f"raw{b}") for b in range(BLOCKS)]
         for b in range(BLOCKS):
             nc.sync.dma_start(raw[b][:], h.rearrange("(p b) s -> b p s", b=BLOCKS)[b])
+        nc.sync.dma_start(offsets[:], offs)
         team_scores = held.tile([T, L], F32, name="team_scores")
         nc.sync.dma_start(team_scores[:], att.rearrange("o (t l) -> (o t) l", l=L))
         gains = held.tile([P, BLOCKS], F32, name="gains")
@@ -48,33 +50,37 @@ def tile_tag_kernel(tc, h, gain, beta, att, offs, out):
 
         top = held.tile([P, T], F32, name="top")
         shifted = held.tile([P, N], F32, name="shifted")
+
+        def weight_step(w):
+            return slice(w * W_PIECE, (w + 1) * W_PIECE), slice(w * W_TEAMS, (w + 1) * W_TEAMS)
+
         for k in range(PIECES):
-            entries = slice(k * PIECE, (k + 1) * PIECE)
-            teams = slice(k * PIECE_TEAMS, (k + 1) * PIECE_TEAMS)
-            nc.vector.tensor_reduce(
-                out=top[:, teams], in_=scores[:, entries].rearrange(BY_TEAM, l=L),
-                axis=AXIS.X, op=ALU.max,
-            )
-        for k in range(PIECES):
-            entries = slice(k * PIECE, (k + 1) * PIECE)
-            teams = slice(k * PIECE_TEAMS, (k + 1) * PIECE_TEAMS)
-            nc.vector.tensor_tensor(
-                out=shifted[:, entries].rearrange(BY_TEAM, l=L),
-                in0=scores[:, entries].rearrange(BY_TEAM, l=L),
-                in1=top[:, teams].unsqueeze(2).to_broadcast([P, PIECE_TEAMS, L]),
-                op=ALU.subtract,
-            )
+            steps_of_piece = range(k * PIECE // W_PIECE, (k + 1) * PIECE // W_PIECE)
+            for w in steps_of_piece:
+                entries, teams = weight_step(w)
+                nc.vector.tensor_reduce(
+                    out=top[:, teams], in_=scores[:, entries].rearrange(BY_TEAM, l=L),
+                    axis=AXIS.X, op=ALU.max,
+                )
+            for w in steps_of_piece:
+                entries, teams = weight_step(w)
+                nc.vector.tensor_tensor(
+                    out=shifted[:, entries].rearrange(BY_TEAM, l=L),
+                    in0=scores[:, entries].rearrange(BY_TEAM, l=L),
+                    in1=top[:, teams].unsqueeze(2).to_broadcast([P, W_TEAMS, L]),
+                    op=ALU.subtract,
+                )
 
         relu = [held.tile([P, S], F32, name=f"relu{b}") for b in range(BLOCKS)]
         sums = held.tile([P, BLOCKS], F32, name="sums")
-        for b in range(BLOCKS):
-            nc.scalar.activation(
-                out=relu[b][:], in_=raw[b][:], func=ACT.Relu, accum_out=sums[:, b : b + 1]
-            )
         expd = held.tile([P, N], F32, name="expd")
-        for k in range(PIECES):
-            entries = slice(k * PIECE, (k + 1) * PIECE)
-            nc.scalar.activation(out=expd[:, entries], in_=shifted[:, entries], func=ACT.Exp)
+        for i in range(BLOCKS):
+            nc.scalar.activation(
+                out=relu[i][:], in_=raw[i][:], func=ACT.Relu, accum_out=sums[:, i : i + 1]
+            )
+            for w in range(i * PIECE // W_PIECE, (i + 1) * PIECE // W_PIECE):
+                entries, teams = weight_step(w)
+                nc.scalar.activation(out=expd[:, entries], in_=shifted[:, entries], func=ACT.Exp)
 
         team_minus_top = held.tile([T, 1], F32, name="team_minus_top")
         nc.vector.tensor_reduce(

@@ -39,12 +39,17 @@ def tile_tag_kernel(tc, h, gain, beta, att, offs, out):
         nc.sync.dma_start(gains[:], gain.rearrange("(p b) o -> p (b o)", b=BLOCKS))
         nc.sync.dma_start(betas[:], beta.rearrange("(p b) o -> p (b o)", b=BLOCKS))
 
+        minus_gains = held.tile([P, BLOCKS], F32, name="minus_gains")
+        nc.gpsimd.tensor_scalar(
+            out=minus_gains[:], in0=gains[:], scalar1=-1.0, scalar2=None, op0=ALU.mult
+        )
+
         minus_half = held.tile([P, BLOCKS], F32, name="minus_half")
         nc.gpsimd.memset(minus_half[:], -0.5)
         eps = held.tile([P, 1], F32, name="eps")
         nc.gpsimd.memset(eps[:], EPS)
-        ones = held.tile([T, P], F32, name="ones")
-        nc.gpsimd.memset(ones[:], 1.0)
+        all_s = held.tile([T, P], F32, name="all_s")
+        nc.gpsimd.memset(all_s[:], float(S))
         identity = held.tile([T, T], F32, name="identity")
         make_identity(nc, identity[:])
 
@@ -72,11 +77,12 @@ def tile_tag_kernel(tc, h, gain, beta, att, offs, out):
                 )
 
         relu = [held.tile([P, S], F32, name=f"relu{b}") for b in range(BLOCKS)]
-        sums = held.tile([P, BLOCKS], F32, name="sums")
+        means = held.tile([P, BLOCKS], F32, name="means")
         expd = held.tile([P, N], F32, name="expd")
         for i in range(BLOCKS):
             nc.scalar.activation(
-                out=relu[i][:], in_=raw[i][:], func=ACT.Relu, accum_out=sums[:, i : i + 1]
+                out=relu[i][:], in_=raw[i][:], func=ACT.Relu, scale=1.0 / S,
+                accum_out=means[:, i : i + 1],
             )
             for w in range(i * PIECE // W_PIECE, (i + 1) * PIECE // W_PIECE):
                 entries, teams = weight_step(w)
@@ -93,22 +99,19 @@ def tile_tag_kernel(tc, h, gain, beta, att, offs, out):
             bias=team_minus_top[:], accum_out=team_den[:],
         )
 
-        minus_mean = held.tile([P, BLOCKS], F32, name="minus_mean")
-        nc.scalar.mul(out=minus_mean[:], in_=sums[:], mul=-1.0 / S)
-
         team_rden = held.tile([T, 1], F32, name="team_rden")
         nc.vector.reciprocal(out=team_rden[:], in_=team_den[:])
         diagonal = held.tile([T, T], F32, name="diagonal")
         nc.scalar.activation(out=diagonal[:], in_=identity[:], func=ACT.Copy, scale=team_rden[:])
         rden = psum.tile([P, T], F32, name="rden")
-        nc.tensor.matmul(rden[:], ones[:], diagonal[:], start=True, stop=True)
+        nc.tensor.matmul(rden[:], all_s[:], diagonal[:], start=True, stop=True)
 
         squares = held.tile([P, BLOCKS], F32, name="squares")
         for b in range(BLOCKS):
             centred_sq = held.tile([P, S], F32, name=f"centred_sq{b}")
             nc.scalar.activation(
                 out=centred_sq[:], in_=relu[b][:], func=ACT.Square,
-                bias=minus_mean[:, b : b + 1], accum_out=squares[:, b : b + 1],
+                scale=-float(S), bias=means[:, b : b + 1], accum_out=squares[:, b : b + 1],
             )
         rstd = held.tile([P, BLOCKS], F32, name="rstd")
         minus_mean_gain = held.tile([P, BLOCKS], F32, name="minus_mean_gain")
@@ -116,7 +119,7 @@ def tile_tag_kernel(tc, h, gain, beta, att, offs, out):
         nc.scalar.activation(
             out=var_eps[:], in_=squares[:], func=ACT.Identity, scale=1.0 / S, bias=eps[:]
         )
-        nc.gpsimd.tensor_tensor(out=minus_mean_gain[:], in0=minus_mean[:], in1=gains[:], op=ALU.mult)
+        nc.gpsimd.tensor_tensor(out=minus_mean_gain[:], in0=means[:], in1=minus_gains[:], op=ALU.mult)
         nc.gpsimd.tensor_tensor(out=rstd[:], in0=var_eps[:], in1=minus_half[:], op=ALU.pow)
         shift = held.tile([P, BLOCKS], F32, name="shift")
         for b in range(BLOCKS):

@@ -119,8 +119,13 @@ def tile_tag_kernel(tc, h, gain, beta, att, offs, out):
         nc.scalar.activation(
             out=var_eps[:], in_=squares[:], func=ACT.Identity, scale=1.0 / S, bias=eps[:]
         )
-        nc.gpsimd.tensor_tensor(out=minus_mean_gain[:], in0=means[:], in1=minus_gains[:], op=ALU.mult)
         nc.gpsimd.tensor_tensor(out=rstd[:], in0=var_eps[:], in1=minus_half[:], op=ALU.pow)
+        for b in range(BLOCKS):
+            block = slice(b, b + 1)
+            nc.scalar.activation(
+                out=minus_mean_gain[:, block], in_=means[:, block], func=ACT.Copy,
+                scale=minus_gains[:, block],
+            )
         shift = held.tile([P, BLOCKS], F32, name="shift")
         for b in range(BLOCKS):
             block = slice(b, b + 1)

@@ -79,14 +79,20 @@ def tile_tag_kernel(tc, h, gain, beta, att, offs, out):
         relu = [held.tile([P, S], F32, name=f"relu{b}") for b in range(BLOCKS)]
         means = held.tile([P, BLOCKS], F32, name="means")
         expd = held.tile([P, N], F32, name="expd")
-        for i in range(BLOCKS):
-            nc.scalar.activation(
-                out=relu[i][:], in_=raw[i][:], func=ACT.Relu, scale=1.0 / S,
-                accum_out=means[:, i : i + 1],
-            )
-            for w in range(i * PIECE // W_PIECE, (i + 1) * PIECE // W_PIECE):
+        def exp_piece(k):
+            for w in range(k * PIECE // W_PIECE, (k + 1) * PIECE // W_PIECE):
                 entries, teams = weight_step(w)
                 nc.scalar.activation(out=expd[:, entries], in_=shifted[:, entries], func=ACT.Exp)
+
+        def relu_block(b):
+            nc.scalar.activation(
+                out=relu[b][:], in_=raw[b][:], func=ACT.Relu, scale=1.0 / S,
+                accum_out=means[:, b : b + 1],
+            )
+
+        relu_block(0)
+        exp_piece(0)
+        relu_block(1)
 
         team_minus_top = held.tile([T, 1], F32, name="team_minus_top")
         nc.vector.tensor_reduce(
@@ -105,6 +111,8 @@ def tile_tag_kernel(tc, h, gain, beta, att, offs, out):
         nc.scalar.activation(out=diagonal[:], in_=identity[:], func=ACT.Copy, scale=team_rden[:])
         rden = psum.tile([P, T], F32, name="rden")
         nc.tensor.matmul(rden[:], all_s[:], diagonal[:], start=True, stop=True)
+
+        exp_piece(1)
 
         squares = held.tile([P, BLOCKS], F32, name="squares")
         for b in range(BLOCKS):

import concourse.mybir as mybir
from concourse.masks import make_identity

F32 = mybir.dt.float32
U16 = mybir.dt.uint16
ALU = mybir.AluOpType
ACT = mybir.ActivationFunctionType
AXIS = mybir.AxisListType

P = 128
C, S, T, L, N = 256, 256, 32, 16, 512
EPS = 1e-5
BLOCKS = C // P
PIECE = S
PIECES = N // PIECE
PIECE_TEAMS = PIECE // L
W_PIECE = 128
W_TEAMS = W_PIECE // L
BY_TEAM = "p (t l) -> p t l"


def tile_tag_kernel(tc, h, gain, beta, att, offs, out):
    nc = tc.nc
    with (
        tc.tile_pool(name="held", bufs=1) as held,
        tc.psum_pool(name="psum", bufs=1) as psum,
    ):
        offsets = held.tile([P, N // 16], U16, name="offsets")
        scores = held.tile([P, N], F32, name="scores")
        nc.sync.dma_start(scores[:], att.broadcast_to([P, N]))
        raw = [held.tile([P, S], F32, name=f"raw{b}") for b in range(BLOCKS)]
        for b in range(BLOCKS):
            nc.sync.dma_start(raw[b][:], h.rearrange("(p b) s -> b p s", b=BLOCKS)[b])
        nc.sync.dma_start(offsets[:], offs)
        team_scores = held.tile([T, L], F32, name="team_scores")
        nc.sync.dma_start(team_scores[:], att.rearrange("o (t l) -> (o t) l", l=L))
        gains = held.tile([P, BLOCKS], F32, name="gains")
        betas = held.tile([P, BLOCKS], F32, name="betas")
        nc.sync.dma_start(gains[:], gain.rearrange("(p b) o -> p (b o)", b=BLOCKS))
        nc.sync.dma_start(betas[:], beta.rearrange("(p b) o -> p (b o)", b=BLOCKS))

        minus_gains = held.tile([P, BLOCKS], F32, name="minus_gains")
        nc.gpsimd.tensor_scalar(
            out=minus_gains[:], in0=gains[:], scalar1=-1.0, scalar2=None, op0=ALU.mult
        )

        minus_half = held.tile([P, BLOCKS], F32, name="minus_half")
        nc.gpsimd.memset(minus_half[:], -0.5)
        eps = held.tile([P, 1], F32, name="eps")
        nc.gpsimd.memset(eps[:], EPS)
        all_s = held.tile([T, P], F32, name="all_s")
        nc.gpsimd.memset(all_s[:], float(S))
        identity = held.tile([T, T], F32, name="identity")
        make_identity(nc, identity[:])

        top = held.tile([P, T], F32, name="top")
        shifted = held.tile([P, N], F32, name="shifted")

        def weight_step(w):
            return slice(w * W_PIECE, (w + 1) * W_PIECE), slice(w * W_TEAMS, (w + 1) * W_TEAMS)

        for k in range(PIECES):
            steps_of_piece = range(k * PIECE // W_PIECE, (k + 1) * PIECE // W_PIECE)
            for w in steps_of_piece:
                entries, teams = weight_step(w)
                nc.vector.tensor_reduce(
                    out=top[:, teams], in_=scores[:, entries].rearrange(BY_TEAM, l=L),
                    axis=AXIS.X, op=ALU.max,
                )
            for w in steps_of_piece:
                entries, teams = weight_step(w)
                nc.vector.tensor_tensor(
                    out=shifted[:, entries].rearrange(BY_TEAM, l=L),
                    in0=scores[:, entries].rearrange(BY_TEAM, l=L),
                    in1=top[:, teams].unsqueeze(2).to_broadcast([P, W_TEAMS, L]),
                    op=ALU.subtract,
                )

        relu = [held.tile([P, S], F32, name=f"relu{b}") for b in range(BLOCKS)]
        means = held.tile([P, BLOCKS], F32, name="means")
        expd = held.tile([P, N], F32, name="expd")
        def exp_piece(k):
            for w in range(k * PIECE // W_PIECE, (k + 1) * PIECE // W_PIECE):
                entries, teams = weight_step(w)
                nc.scalar.activation(out=expd[:, entries], in_=shifted[:, entries], func=ACT.Exp)

        def relu_block(b):
            nc.scalar.activation(
                out=relu[b][:], in_=raw[b][:], func=ACT.Relu, scale=1.0 / S,
                accum_out=means[:, b : b + 1],
            )

        relu_block(0)
        exp_piece(0)
        relu_block(1)

        team_minus_top = held.tile([T, 1], F32, name="team_minus_top")
        nc.vector.tensor_reduce(
            out=team_minus_top[:], in_=team_scores[:], axis=AXIS.X, op=ALU.max, negate=True
        )
        team_expd = held.tile([T, L], F32, name="team_expd")
        team_den = held.tile([T, 1], F32, name="team_den")
        nc.scalar.activation(
            out=team_expd[:], in_=team_scores[:], func=ACT.Exp,
            bias=team_minus_top[:], accum_out=team_den[:],
        )

        team_rden = held.tile([T, 1], F32, name="team_rden")
        nc.vector.reciprocal(out=team_rden[:], in_=team_den[:])
        diagonal = held.tile([T, T], F32, name="diagonal")
        nc.scalar.activation(out=diagonal[:], in_=identity[:], func=ACT.Copy, scale=team_rden[:])
        rden = psum.tile([P, T], F32, name="rden")
        nc.tensor.matmul(rden[:], all_s[:], diagonal[:], start=True, stop=True)

        exp_piece(1)

        squares = held.tile([P, BLOCKS], F32, name="squares")
        for b in range(BLOCKS):
            centred_sq = held.tile([P, S], F32, name=f"centred_sq{b}")
            nc.scalar.activation(
                out=centred_sq[:], in_=relu[b][:], func=ACT.Square,
                scale=-float(S), bias=means[:, b : b + 1], accum_out=squares[:, b : b + 1],
            )
        rstd = held.tile([P, BLOCKS], F32, name="rstd")
        minus_mean_gain = held.tile([P, BLOCKS], F32, name="minus_mean_gain")
        var_eps = held.tile([P, BLOCKS], F32, name="var_eps")
        nc.scalar.activation(
            out=var_eps[:], in_=squares[:], func=ACT.Identity, scale=1.0 / S, bias=eps[:]
        )
        nc.gpsimd.tensor_tensor(out=rstd[:], in0=var_eps[:], in1=minus_half[:], op=ALU.pow)
        for b in range(BLOCKS):
            block = slice(b, b + 1)
            nc.scalar.activation(
                out=minus_mean_gain[:, block], in_=means[:, block], func=ACT.Copy,
                scale=minus_gains[:, block],
            )
        shift = held.tile([P, BLOCKS], F32, name="shift")
        for b in range(BLOCKS):
            block = slice(b, b + 1)
            nc.scalar.activation(
                out=shift[:, block], in_=rstd[:, block], func=ACT.Identity,
                scale=minus_mean_gain[:, block], bias=betas[:, block],
            )

        picked = held.tile([P, BLOCKS, N], F32, name="picked")
        summed = held.tile([P, BLOCKS, T], F32, name="summed")

        def sum_teams(b, k):
            nc.vector.tensor_reduce(
                out=summed[:, b, k * PIECE_TEAMS : (k + 1) * PIECE_TEAMS],
                in_=picked[:, b, k * PIECE : (k + 1) * PIECE].rearrange(BY_TEAM, l=L),
                axis=AXIS.X, op=ALU.add,
            )

        steps = [(b, k) for b in range(BLOCKS) for k in range(PIECES)]
        for i, (b, k) in enumerate(steps):
            nc.vector.tensor_tensor(
                out=picked[:, b, k * PIECE : (k + 1) * PIECE],
                in0=relu[b][:].indirect(offsets[:, k * PIECE // 16 : (k + 1) * PIECE // 16]),
                in1=expd[:, k * PIECE : (k + 1) * PIECE],
                op=ALU.mult,
            )
            if i > 0:
                sum_teams(*steps[i - 1])
        sum_teams(*steps[-1])

        normed = held.tile([P, BLOCKS, T], F32, name="normed")
        result = held.tile([P, BLOCKS, T], F32, name="result")
        for b in range(BLOCKS):
            nc.vector.scalar_tensor_tensor(
                out=normed[:, b, :], in0=summed[:, b, :], scalar=rstd[:, b : b + 1], in1=rden[:],
                op0=ALU.mult, op1=ALU.mult,
            )
        for b in range(BLOCKS):
            nc.vector.tensor_scalar(
                out=result[:, b, :], in0=normed[:, b, :],
                scalar1=gains[:, b : b + 1], scalar2=shift[:, b : b + 1],
                op0=ALU.mult, op1=ALU.add,
            )
        nc.sync.dma_start(out.rearrange("(p b) t -> p b t", b=BLOCKS), result[:])
